import numpy as np
import ml_dtypes


def mxq(x, axis, fmt="e4m3"):
    dtype, down = {"e4m3": (ml_dtypes.float8_e4m3fn, 7), "e5m2": (ml_dtypes.float8_e5m2, 14)}[fmt]
    v = np.moveaxis(np.asarray(x, np.float32).astype(ml_dtypes.bfloat16).astype(np.float64), axis, -1)
    blocks = v.reshape(v.shape[:-1] + (-1, 32))
    amax = np.abs(blocks).max(-1, keepdims=True)
    byte = np.maximum(np.where(amax > 0, np.frexp(amax)[1] - 1 + 127, 0) - down, 1)
    scale = np.exp2(byte - 127.0)
    codes = (blocks / scale).astype(np.float32).astype(dtype).astype(np.float64)
    return np.moveaxis((codes * scale).reshape(v.shape), -1, axis)


WIDE = False


def mx_kscale(k):
    if not WIDE:
        return np.ones(k)
    levels = np.array([10, -10, 5, -5, 0])
    if k % 512:
        return np.exp2(np.random.permutation(np.resize(levels, k // 32))).repeat(32)
    a = np.empty((k // 512, 16))
    for p in range(k // 512):
        a[p, :8] = np.random.permutation(np.resize(levels, 8))
        for g in range(8):
            far = levels[np.abs(levels - a[p, g]) >= 10]
            a[p, g + 8] = far[np.random.randint(len(far))]
    return np.exp2(a.ravel()).repeat(32)


BF16 = ml_dtypes.bfloat16


def bf(x):
    return np.asarray(x, np.float32).astype(BF16)


def f64(x):
    return np.asarray(x).astype(np.float64)


B, S, D, H, QK = 1, 1024, 1024, 2048, 128
R = np.sqrt(0.1 * S / np.sqrt(QK))


def silu(a):
    return a / (1.0 + np.exp(-a))


def draw0():
    u = np.exp2(np.round(np.log2(mx_kscale(S)) / 2))
    t = mx_kscale(H)
    return {
        "q": bf(np.random.standard_normal((B, S, QK)) * R),
        "k": bf(np.random.standard_normal((B, S, QK)) * R * u[:, None]),
        "v": bf(silu(np.random.standard_normal((B, S, H))) / (u * u)[:, None]),
        "gate": bf(silu(np.random.standard_normal((B, S, H))) * t),
        "W_out": bf(np.random.standard_normal((D, H)) / np.sqrt(H) / t),
        "b_out": bf(np.random.standard_normal(D) * 0.1),
        "x": bf(np.random.standard_normal((B, S, D))),
    }


def core(q, k, v, gate, W_out, b_out, x):
    sim = f64(q) @ f64(k).transpose(0, 2, 1) / S
    A = np.square(np.maximum(sim, 0.0))
    V = (mxq(A, 2, "e4m3") @ mxq(f64(v), 1, "e4m3")) * f64(gate)
    return (mxq(V, 2, "e4m3") @ mxq(f64(W_out), 1, "e4m3").T) + f64(b_out) + f64(x)


def e4m3fn_bytes(y):
    return np.clip(np.asarray(y, np.float64), -448.0, 448.0).astype(np.float32).astype(ml_dtypes.float8_e4m3fn).view(np.uint8)


def e4m3fn_values(b):
    return np.asarray(b, np.uint8).view(ml_dtypes.float8_e4m3fn).astype(np.float64)


def setup_inputs():
    d = draw0()
    x0 = np.asarray(d['v']).astype(np.float64)
    s = (np.max(np.abs(x0), axis=(0, 2), keepdims=True) / 448.0).astype(np.float32)
    out = {}
    for k, v in d.items():
        if k == 'v':
            out['v_bytes'] = e4m3fn_bytes(x0 / s.astype(np.float64))
            out['v_scale'] = s
        else:
            out[k] = v
    return out


def reference(q, k, v_bytes, v_scale, gate, W_out, b_out, x):
    return core(q, k, e4m3fn_values(v_bytes) * v_scale.astype(np.float64), gate, W_out, b_out, x)

@@ -1,0 +1,632 @@
+from contextlib import ExitStack
+
+import concourse.mybir as mybir
+from concourse.masks import make_identity
+
+S, D, H, QK = 1024, 1024, 2048, 128
+P = 128
+F32 = mybir.dt.float32
+BF16 = mybir.dt.bfloat16
+U32 = mybir.dt.uint32
+U8 = mybir.dt.uint8
+FP8 = mybir.dt.float8_e4m3fn
+X4 = mybir.dt.float8_e4m3fn_x4
+ACT = mybir.ActivationFunctionType
+ALU = mybir.AluOpType
+
+FLOPS = 2 * S * S * QK + 2 * S * S * H + 2 * S * H * D
+
+QT = S // P
+KG = S // 512
+HC = H // 512
+DB = D // P
+
+
+def tile_gau_pa_kernel(tc, q, k, v_bytes, v_scale, gate, W_out, b_out, x, out):
+    nc = tc.nc
+    with ExitStack() as ctx:
+        const = ctx.enter_context(tc.tile_pool(name="const", bufs=1))
+        keep = ctx.enter_context(tc.tile_pool(name="keep", bufs=1))
+        work = ctx.enter_context(tc.tile_pool(name="work", bufs=2))
+        psum = ctx.enter_context(tc.psum_pool(name="psum", bufs=4))
+        ctx.enter_context(tc.manual_schedule())
+
+        q_view = q.rearrange("b (p i) d -> p (b i) d", i=QT)
+        k_view = k.rearrange("b (g m t) d -> m (b g) t d", g=KG, t=4)
+        v_view = v_bytes.rearrange("b (g p t) n -> (b g) p t n", p=P, t=4)
+        s_view = v_scale.rearrange("b (g p t) o -> p (b g) (t o)", p=P, t=4)
+        gate_view = gate.rearrange("b (p i) h -> p (b i) h", i=QT)
+        x_view = x.rearrange("b (p i) d -> p (b i) d", i=QT)
+        out_view = out.rearrange("b (p i) d -> p (b i) d", i=QT)
+        w_view = W_out.rearrange("(j p) h -> j p h", p=P)
+
+        q_sb = const.tile([P, QT, QK], BF16, name="q_sb")
+        k_sb = const.tile([P, KG, 4, QK], BF16, name="k_sb")
+        v_sc = const.tile([P, KG, 4], F32, name="v_sc")
+        b_row = const.tile([P, D], BF16, name="b_row")
+        ident_b = const.tile([P, P], BF16, name="ident_b")
+        ident_f = const.tile([P, P], F32, name="ident_f")
+        ones = const.tile([P, P], BF16, name="ones")
+
+        make_identity(nc, ident_b[:])
+        make_identity(nc, ident_f[:])
+        nc.gpsimd.memset(b_row[:], 0.0)
+        nc.gpsimd.memset(ones[:], 1.0)
+        warm = const.tile([P, 1], F32, name="warm")
+        nc.vector.memset(warm[:], 0.0)
+        nc.scalar.activation(out=warm[:], in_=warm[:], func=ACT.Square)
+
+
+        v_raw = {}
+        w_raw = {}
+        gates = {}
+        xs = {}
+
+        def load_v(c):
+            for g in range(KG):
+                t = keep.tile([P, 4, 512], U8, name="v_raw_%d_%d" % (c, g), align_bytes=64)
+                nc.sync.dma_start(out=t[:], in_=v_view[g][:, :, c * 512 : (c + 1) * 512])
+                v_raw[c, g] = t
+
+        def load_q():
+            nc.sync.dma_start(out=q_sb[:], in_=q_view)
+
+        def load_k():
+            nc.sync.dma_start(out=k_sb[:], in_=k_view)
+
+        nc.sync.dma_start(out=v_sc[:], in_=s_view)
+
+        def load_w(j):
+            t = work.tile([P, H], BF16, name="w_raw_%d" % j, tag="w_raw", bufs=4)
+            nc.sync.dma_start(out=t[:], in_=w_view[j])
+            w_raw[j] = t
+
+        def load_gate(i):
+            t = work.tile([P, H], BF16, name="gate_%d" % i, tag="gate", bufs=4)
+            nc.sync.dma_start(out=t[:], in_=gate_view[:, i, :])
+            gates[i] = t
+
+        def load_x(i):
+            t = work.tile([P, D], BF16, name="x_%d" % i, tag="x", bufs=3)
+            nc.sync.dma_start(out=t[:], in_=x_view[:, i, :])
+            xs[i] = t
+
+        qT = const.tile([P, S], BF16, name="qT")
+        kT = const.tile([P, S], BF16, name="kT")
+
+        qk_ps = {}
+
+        def flip_q(half):
+            ps = psum.tile([P, 4, P], BF16, name="flip", tag="misc", bufs=4)
+            for t in range(4):
+                nc.tensor.transpose(ps[:, t, :], q_sb[:, 4 * half + t, :], ident_b[:])
+            qk_ps["q", half] = ps
+
+        def flip_k(half):
+            ps = psum.tile([P, 4, P], BF16, name="flip", tag="misc", bufs=4)
+            for t in range(4):
+                nc.tensor.transpose(ps[:, t, :], k_sb[:, half, t, :], ident_b[:])
+            qk_ps["k", half] = ps
+
+        def flop_q(half, copy):
+            copy(out=qT[:, half * 512 : (half + 1) * 512], in_=qk_ps["q", half][:].rearrange("p t m -> p (t m)"))
+
+        def flop_k(half, copy):
+            copy(out=kT[:, half * 512 : (half + 1) * 512], in_=qk_ps["k", half][:].rearrange("p t m -> p (t m)"))
+
+        r_t = {}
+        a_codes = {}
+        a_scales = {}
+        sims = {}
+
+        def sim_mm(i, g):
+            ps = psum.tile([P, 4, P], F32, name="sim", tag="misc", bufs=4)
+            for t in range(4):
+                o = (4 * g + t) * P
+                nc.tensor.matmul(ps[:, t, :], lhsT=kT[:, o : o + P], rhs=qT[:, i * P : (i + 1) * P], start=True, stop=True)
+            sims[i, g] = ps
+
+        def relu(i, g):
+            if i not in r_t:
+                r_t[i] = work.tile([P, S], F32, name="r", tag="r", bufs=2)
+            nc.scalar.activation(
+                out=r_t[i][:, g * 512 : (g + 1) * 512].rearrange("p (q t) -> p q t", t=4),
+                in_=sims[i, g][:].rearrange("p t q -> p q t"),
+                func=ACT.Relu,
+                scale=1.0 / S,
+            )
+
+        def square(i):
+            a = work.tile([P, S], BF16, name="a", tag="a", bufs=2, align_bytes=64)
+            nc.scalar.activation(out=a[:], in_=r_t[i][:], func=ACT.Square)
+            r_t[i] = a
+
+        def a_quant(i):
+            c = keep.tile([P, KG * P], U32, name="a_codes_%d" % i, align_bytes=64)
+            s = keep.tile([P, KG * P], U8, name="a_scales_%d" % i, align_bytes=64)
+            nc.vector.quantize_mx(out=c[:].bitcast(X4), scales=s[:], in_=r_t[i][:])
+            a_codes[i] = c
+            a_scales[i] = s
+
+        v_wide = {}
+        v_il = {}
+        v_codes = {}
+        v_scales = {}
+
+        def v_widen(c, g, t, on_vector):
+            if (c, g) not in v_wide:
+                v_wide[c, g] = work.tile([P, 4, 512], BF16, name="v_wide", tag="v_wide", bufs=3)
+            w = v_wide[c, g]
+            src = v_raw[c, g][:, t, :].bitcast(FP8)
+            sc = v_sc[:, g, t : t + 1]
+            if on_vector:
+                nc.vector.tensor_scalar(out=w[:, t, :], in0=src, scalar1=sc, scalar2=None, op0=ALU.mult)
+            else:
+                nc.scalar.activation(out=w[:, t, :], in_=src, func=ACT.Copy, scale=sc)
+
+        def v_interleave(c, g):
+            t = work.tile([P, 2048], BF16, name="v_il", tag="v_il", bufs=2, align_bytes=64)
+            nc.vector.tensor_copy(
+                out=t[:].rearrange("p (c i t) -> p c t i", t=4, i=4),
+                in_=v_wide[c, g][:].rearrange("p t (c i) -> p c t i", i=4),
+            )
+            v_il[c, g] = t
+
+        def v_quant(c, g):
+            co = keep.tile([P, 512], U32, name="v_codes_%d_%d" % (c, g), align_bytes=64)
+            sc = keep.tile([P, 512], U8, name="v_scales_%d_%d" % (c, g), align_bytes=64)
+            nc.vector.quantize_mx(out=co[:].bitcast(X4), scales=sc[:], in_=v_il[c, g][:])
+            v_codes[c, g] = co
+            v_scales[c, g] = sc
+
+        w_il = {}
+        w_codes = {}
+        w_scales = {}
+
+        w_ps = {}
+
+        def w_flip(j, pair):
+            words = w_raw[j][:].bitcast(F32)
+            ps = psum.tile([P, 4, P], F32, name="w_flip", tag="misc", bufs=4)
+            for c2 in range(2):
+                for u in range(2):
+                    base = 256 * (2 * pair + c2)
+                    nc.tensor.transpose(ps[:, 2 * c2 + u, :], words[:, base + u : base + 256 : 2], ident_f[:])
+            w_ps[j, pair] = ps
+
+        def w_evac(j, pair, copy):
+            half, jj = divmod(j, 4)
+            if (half, pair) not in w_il:
+                w_il[half, pair] = work.tile([P, 2 * 512 * 4], BF16, name="w_il", tag="w_il", bufs=3, align_bytes=64)
+            dst = w_il[half, pair][:].bitcast(F32).rearrange("p (c d u) -> p c d u", c=2, u=2)[:, :, jj * P : (jj + 1) * P, :]
+            copy(out=dst, in_=w_ps[j, pair][:].rearrange("p (c u) d -> p c d u", u=2))
+
+        def w_quant(half, c):
+            co = keep.tile([P, 512], U32, name="w_codes_%d_%d" % (half, c), align_bytes=64)
+            sc = keep.tile([P, 512], U8, name="w_scales_%d_%d" % (half, c), align_bytes=64)
+            src = w_il[half, c // 2][:, (c % 2) * 2048 : (c % 2 + 1) * 2048]
+            nc.vector.quantize_mx(out=co[:].bitcast(X4), scales=sc[:], in_=src)
+            w_codes[half, c] = co
+            w_scales[half, c] = sc
+
+        vb = {}
+        accs = {}
+
+        def mm1(i, c):
+            acc = psum.tile([P, 512], F32, name="acc", tag="acc", bufs=4)
+            for g in range(KG):
+                cols = slice(g * P, (g + 1) * P)
+                nc.tensor.matmul_mx(
+                    out=acc[:],
+                    lhsT=a_codes[i][:, cols].bitcast(X4),
+                    lhsT_scale=a_scales[i][:, cols],
+                    rhs=v_codes[c, g][:].bitcast(X4),
+                    rhs_scale=v_scales[c, g][:],
+                    start=(g == 0),
+                    stop=(g == KG - 1),
+                )
+            accs[i, c] = acc
+
+        def gate_mul(i, c):
+            if i not in vb:
+                vb[i] = work.tile([P, H], BF16, name="vb", tag="vb", bufs=4)
+            cols = slice(c * 512, (c + 1) * 512)
+            nc.vector.tensor_tensor(
+                out=vb[i][:, cols].rearrange("p (u w e) -> p u w e", u=2, e=2),
+                in0=accs[i, c][:].rearrange("p (w u e) -> p u w e", u=2, e=2),
+                in1=gates[i][:, cols].rearrange("p (w u e) -> p u w e", u=2, e=2),
+                op=ALU.mult,
+            )
+
+        vg = {}
+        vt_codes = {}
+        vt_scales = {}
+
+        vps = {}
+
+        def v_flip(i, pair):
+            words = vb[i][:].bitcast(F32)
+            ps = psum.tile([P, 4, P], F32, name="v_flip", tag="misc", bufs=4)
+            for n in range(4):
+                base = (4 * pair + n) * P
+                nc.tensor.transpose(ps[:, n, :], words[:, base : base + P], ident_f[:])
+            vps[i, pair] = ps
+
+        def v_evac(i, pair, copy):
+            if i not in vg:
+                vg[i] = work.tile([P, H], BF16, name="vg", tag="vg", bufs=2, align_bytes=64)
+            dst = vg[i][:].bitcast(F32).rearrange("p (c q u) -> p c q u", c=HC, u=2)
+            copy(out=dst[:, 2 * pair : 2 * pair + 2], in_=vps[i, pair][:].rearrange("p (c u) q -> p c q u", u=2))
+
+        def v_t_quant(i):
+            co = work.tile([P, 512], U32, name="vt_codes", tag="vt_codes", bufs=8, align_bytes=64)
+            sc = work.tile([P, 512], U8, name="vt_scales", tag="vt_scales", bufs=8, align_bytes=64)
+            nc.vector.quantize_mx(out=co[:].bitcast(X4), scales=sc[:], in_=vg[i][:])
+            vt_codes[i] = co
+            vt_scales[i] = sc
+
+        xb = {}
+        outs = {}
+
+        def make_xb(i):
+            xb[i] = work.tile([P, D], F32, name="xb", tag="xb", bufs=2)
+            nc.gpsimd.tensor_tensor(out=xb[i][:], in0=xs[i][:], in1=b_all[:], op=ALU.add)
+
+        def mm2(i, halves=(0, 1)):
+            for half in halves:
+                acc = psum.tile([P, 512], F32, name="acc", tag="acc", bufs=4)
+                for c in range(HC):
+                    cols = slice(c * P, (c + 1) * P)
+                    nc.tensor.matmul_mx(
+                        out=acc[:],
+                        lhsT=vt_codes[i][:, cols].bitcast(X4),
+                        lhsT_scale=vt_scales[i][:, cols],
+                        rhs=w_codes[half, c][:].bitcast(X4),
+                        rhs_scale=w_scales[half, c][:],
+                        start=(c == 0),
+                        stop=(c == HC - 1),
+                    )
+                outs[i, half] = acc
+
+        o_t = {}
+
+        def finish(i, half):
+            cols = slice(half * 512, (half + 1) * 512)
+            o = work.tile([P, 512], F32, name="o", tag="o", bufs=5)
+            nc.vector.tensor_tensor(out=o[:], in0=outs[i, half][:], in1=xb[i][:, cols], op=ALU.add)
+            nc.sync.dma_start(out=out_view[:, i, cols], in_=o[:])
+
+        vcopy = nc.vector.tensor_copy
+        scopy = nc.scalar.copy
+        b_all = const.tile([P, D], BF16, name="b_all")
+
+        def spread_bias():
+            for half in range(2):
+                cols = slice(half * 512, (half + 1) * 512)
+                ps = psum.tile([P, 512], F32, name="bias", tag="acc", bufs=4)
+                nc.tensor.matmul(ps[:], lhsT=ones[:], rhs=b_row[:, cols], start=True, stop=True)
+                nc.scalar.copy(out=b_all[:, cols], in_=ps[:])
+
+        def load_bias():
+            nc.sync.dma_start(out=b_row[0:1, :], in_=b_out.rearrange("(o d) -> o d", o=1))
+
+        load_v(0)
+        load_w(0)
+        load_bias()
+        load_v(1)
+        v_widen(0, 1, 0, True)
+        v_widen(0, 1, 2, False)
+        load_w(1)
+        v_widen(0, 1, 1, True)
+        v_widen(0, 1, 3, False)
+        v_widen(0, 0, 0, True)
+        v_widen(0, 0, 1, True)
+        v_widen(0, 0, 2, False)
+        w_flip(0, 0)
+        v_interleave(0, 1)
+        load_q()
+        v_widen(0, 0, 3, False)
+        w_flip(0, 1)
+        load_k()
+        w_evac(0, 0, scopy)
+        load_w(2)
+        v_interleave(0, 0)
+        w_evac(0, 1, scopy)
+        v_widen(1, 1, 2, False)
+        load_w(3)
+        w_flip(1, 0)
+        v_widen(1, 1, 3, False)
+        v_widen(1, 1, 0, True)
+        w_flip(1, 1)
+        v_widen(1, 1, 1, True)
+        v_widen(1, 0, 2, False)
+        v_quant(0, 1)
+        load_v(2)
+        v_widen(1, 0, 3, False)
+        v_widen(1, 0, 0, True)
+        v_widen(1, 0, 1, True)
+        w_evac(1, 0, scopy)
+        v_quant(0, 0)
+        w_flip(2, 0)
+        w_evac(1, 1, scopy)
+        load_w(4)
+        v_interleave(1, 1)
+        w_flip(2, 1)
+        w_evac(2, 0, scopy)
+        w_flip(3, 0)
+        w_evac(2, 1, scopy)
+        load_w(5)
+        v_interleave(1, 0)
+        w_flip(3, 1)
+        w_evac(3, 0, scopy)
+        flip_q(0)
+        w_evac(3, 1, scopy)
+        flip_k(0)
+        load_w(6)
+        flip_k(1)
+        w_quant(0, 0)
+        v_widen(2, 1, 1, False)
+        flip_q(1)
+        v_widen(2, 1, 0, True)
+        v_widen(2, 1, 2, False)
+        load_v(3)
+        v_quant(1, 1)
+        v_widen(2, 1, 3, False)
+        v_widen(2, 0, 0, True)
+        v_widen(2, 0, 1, False)
+        v_quant(1, 0)
+        load_w(7)
+        v_widen(2, 0, 2, False)
+        flop_k(0, vcopy)
+        flop_q(1, vcopy)
+        v_widen(2, 0, 3, False)
+        v_interleave(2, 1)
+        load_gate(0)
+        flop_q(0, scopy)
+        flop_k(1, scopy)
+        w_flip(4, 0)
+        w_quant(0, 1)
+        w_flip(4, 1)
+        load_x(0)
+        w_evac(4, 0, scopy)
+        v_interleave(2, 0)
+        sim_mm(0, 0)
+        w_evac(4, 1, scopy)
+        load_gate(1)
+        sim_mm(0, 1)
+        spread_bias()
+        w_flip(5, 0)
+        relu(0, 0)
+        relu(0, 1)
+        v_widen(3, 1, 0, True)
+        load_gate(2)
+        w_flip(5, 1)
+        v_widen(3, 1, 1, True)
+        w_evac(5, 0, scopy)
+        sim_mm(1, 0)
+        v_widen(3, 1, 2, True)
+        v_widen(3, 1, 3, True)
+        sim_mm(1, 1)
+        w_evac(5, 1, scopy)
+        v_quant(2, 1)
+        load_x(1)
+        make_xb(0)
+        w_flip(6, 0)
+        relu(1, 0)
+        v_widen(3, 0, 0, True)
+        load_gate(3)
+        w_flip(6, 1)
+        v_widen(3, 0, 1, True)
+        relu(1, 1)
+        v_widen(3, 0, 2, True)
+        sim_mm(2, 0)
+        v_widen(3, 0, 3, True)
+        square(0)
+        v_quant(2, 0)
+        sim_mm(2, 1)
+        load_x(2)
+        w_quant(0, 2)
+        w_evac(6, 0, scopy)
+        v_interleave(3, 1)
+        make_xb(1)
+        w_evac(6, 1, scopy)
+        w_flip(7, 0)
+        relu(2, 0)
+        w_flip(7, 1)
+        a_quant(0)
+        relu(2, 1)
+        sim_mm(3, 0)
+        v_interleave(3, 0)
+        square(1)
+        sim_mm(3, 1)
+        mm1(0, 0)
+        v_quant(3, 1)
+        mm1(0, 1)
+        w_evac(7, 0, scopy)
+        mm1(0, 2)
+        v_quant(3, 0)
+        w_evac(7, 1, scopy)
+        a_quant(1)
+        relu(3, 0)
+        mm1(0, 3)
+        gate_mul(0, 0)
+        relu(3, 1)
+        sim_mm(4, 0)
+        gate_mul(0, 1)
+        sim_mm(4, 1)
+        square(2)
+        mm1(1, 0)
+        gate_mul(0, 2)
+        mm1(1, 1)
+        gate_mul(0, 3)
+        square(3)
+        mm1(1, 2)
+        a_quant(2)
+        load_gate(4)
+        gate_mul(1, 0)
+        mm1(1, 3)
+        gate_mul(1, 1)
+        v_flip(0, 1)
+        gate_mul(1, 2)
+        v_flip(0, 0)
+        v_evac(0, 1, scopy)
+        mm1(2, 0)
+        gate_mul(1, 3)
+        v_evac(0, 0, scopy)
+        mm1(2, 1)
+        w_quant(0, 3)
+        load_gate(5)
+        relu(4, 0)
+        mm1(2, 2)
+        a_quant(3)
+        relu(4, 1)
+        w_quant(1, 0)
+        mm1(2, 3)
+        load_x(3)
+        gate_mul(2, 0)
+        square(4)
+        sim_mm(5, 0)
+        sim_mm(5, 1)
+        gate_mul(2, 1)
+        mm1(3, 0)
+        gate_mul(2, 2)
+        relu(5, 0)
+        v_flip(1, 1)
+        gate_mul(2, 3)
+        relu(5, 1)
+        v_flip(1, 0)
+        sim_mm(6, 0)
+        v_evac(1, 1, scopy)
+        v_t_quant(0)
+        load_gate(6)
+        sim_mm(6, 1)
+        v_evac(1, 0, scopy)
+        a_quant(4)
+        mm1(3, 1)
+        w_quant(1, 1)
+        square(5)
+        load_x(4)
+        mm1(3, 2)
+        gate_mul(3, 0)
+        mm1(3, 3)
+        gate_mul(3, 1)
+        relu(6, 0)
+        mm1(4, 0)
+        a_quant(5)
+        relu(6, 1)
+        sim_mm(7, 0)
+        w_quant(1, 2)
+        sim_mm(7, 1)
+        square(6)
+        gate_mul(3, 2)
+        mm1(4, 1)
+        v_t_quant(1)
+        v_flip(2, 1)
+        v_flip(2, 0)
+        gate_mul(3, 3)
+        v_evac(2, 1, scopy)
+        mm1(4, 2)
+        gate_mul(4, 0)
+        relu(7, 0)
+        load_gate(7)
+        mm2(0, (0,))
+        w_quant(1, 3)
+        relu(7, 1)
+        a_quant(6)
+        v_evac(2, 0, scopy)
+        gate_mul(4, 1)
+        mm2(0, (1,))
+        square(7)
+        gate_mul(4, 2)
+        finish(0, 0)
+        mm1(4, 3)
+        finish(0, 1)
+        mm1(5, 0)
+        gate_mul(4, 3)
+        mm1(5, 1)
+        make_xb(2)
+        a_quant(7)
+        mm1(5, 2)
+        gate_mul(5, 0)
+        mm2(1, (0,))
+        v_t_quant(2)
+        gate_mul(5, 1)
+        mm2(1, (1,))
+        load_x(5)
+        gate_mul(5, 2)
+        finish(1, 0)
+        mm1(5, 3)
+        finish(1, 1)
+        mm1(6, 0)
+        gate_mul(5, 3)
+        make_xb(3)
+        mm1(6, 1)
+        gate_mul(6, 0)
+        mm1(6, 2)
+        gate_mul(6, 1)
+        mm1(6, 3)
+        gate_mul(6, 2)
+        v_flip(3, 1)
+        gate_mul(6, 3)
+        v_flip(3, 0)
+        load_x(6)
+        v_evac(3, 1, scopy)
+        mm1(7, 0)
+        v_evac(3, 0, scopy)
+        mm1(7, 1)
+        gate_mul(7, 0)
+        mm2(2, (0,))
+        gate_mul(7, 1)
+        mm2(2, (1,))
+        finish(2, 0)
+        mm1(7, 2)
+        finish(2, 1)
+        mm1(7, 3)
+        gate_mul(7, 2)
+        make_xb(4)
+        v_flip(4, 1)
+        v_t_quant(3)
+        v_flip(4, 0)
+        v_evac(4, 1, scopy)
+        gate_mul(7, 3)
+        v_flip(5, 1)
+        v_flip(5, 0)
+        v_evac(4, 0, scopy)
+        v_evac(5, 1, vcopy)
+        mm2(3, (0,))
+        v_evac(5, 0, scopy)
+        v_t_quant(4)
+        load_x(7)
+        mm2(3, (1,))
+        finish(3, 0)
+        v_flip(6, 1)
+        finish(3, 1)
+        v_flip(6, 0)
+        v_evac(6, 1, scopy)
+        v_t_quant(5)
+        v_flip(7, 1)
+        make_xb(5)
+        v_flip(7, 0)
+        v_evac(6, 0, scopy)
+        v_evac(7, 1, vcopy)
+        mm2(4, (0,))
+        v_evac(7, 0, scopy)
+        v_t_quant(6)
+        mm2(4, (1,))
+        finish(4, 0)
+        mm2(5, (0,))
+        finish(4, 1)
+        v_t_quant(7)
+        make_xb(6)
+        mm2(5, (1,))
+        finish(5, 0)
+        mm2(6, (0,))
+        finish(5, 1)
+        make_xb(7)
+        mm2(6, (1,))
+        finish(6, 0)
+        mm2(7, (0,))
+        finish(6, 1)
+        mm2(7, (1,))
+        finish(7, 0)
+        finish(7, 1)

@@ -229,7 +229,7 @@ def tile_gau_pa_kernel(tc, q, k, v_bytes, v_scale, gate, W_out, b_out, x, out):
 
         def gate_mul(i, c):
             if i not in vb:
-                vb[i] = work.tile([P, H], BF16, name="vb", tag="vb", bufs=4)
+                vb[i] = work.tile([P, H], BF16, name="vb", tag="vb", bufs=3)
             cols = slice(c * 512, (c + 1) * 512)
             nc.vector.tensor_tensor(
                 out=vb[i][:, cols].rearrange("p (u w e) -> p u w e", u=2, e=2),
@@ -268,9 +268,10 @@ def tile_gau_pa_kernel(tc, q, k, v_bytes, v_scale, gate, W_out, b_out, x, out):
         xb = {}
         outs = {}
 
-        def make_xb(i):
-            xb[i] = work.tile([P, D], F32, name="xb", tag="xb", bufs=2)
-            nc.gpsimd.tensor_tensor(out=xb[i][:], in0=xs[i][:], in1=b_all[:], op=ALU.add)
+        def make_xb(i, half):
+            cols = slice(half * 512, (half + 1) * 512)
+            xb[i, half] = work.tile([P, 512], F32, name="xb", tag="xb", bufs=4)
+            nc.vector.tensor_tensor(out=xb[i, half][:], in0=xs[i][:, cols], in1=b_all[:, cols], op=ALU.add)
 
         def mm2(i, halves=(0, 1)):
             for half in halves:
@@ -293,7 +294,7 @@ def tile_gau_pa_kernel(tc, q, k, v_bytes, v_scale, gate, W_out, b_out, x, out):
         def finish(i, half):
             cols = slice(half * 512, (half + 1) * 512)
             o = work.tile([P, 512], F32, name="o", tag="o", bufs=5)
-            nc.vector.tensor_tensor(out=o[:], in0=outs[i, half][:], in1=xb[i][:, cols], op=ALU.add)
+            nc.vector.tensor_tensor(out=o[:], in0=outs[i, half][:], in1=xb[i, half][:], op=ALU.add)
             nc.sync.dma_start(out=out_view[:, i, cols], in_=o[:])
 
         vcopy = nc.vector.tensor_copy
@@ -310,323 +311,331 @@ def tile_gau_pa_kernel(tc, q, k, v_bytes, v_scale, gate, W_out, b_out, x, out):
         def load_bias():
             nc.sync.dma_start(out=b_row[0:1, :], in_=b_out.rearrange("(o d) -> o d", o=1))
 
-        load_v(0)
         load_w(0)
+        load_v(0)
         load_bias()
-        load_v(1)
-        v_widen(0, 1, 0, True)
-        v_widen(0, 1, 2, False)
         load_w(1)
-        v_widen(0, 1, 1, True)
-        v_widen(0, 1, 3, False)
+        load_v(1)
+        load_w(2)
+        load_w(3)
+        load_v(2)
+        load_q()
+        load_k()
+        w_flip(0, 0)
+        w_flip(0, 1)
         v_widen(0, 0, 0, True)
         v_widen(0, 0, 1, True)
         v_widen(0, 0, 2, False)
-        w_flip(0, 0)
-        v_interleave(0, 1)
-        load_q()
         v_widen(0, 0, 3, False)
-        w_flip(0, 1)
-        load_k()
-        w_evac(0, 0, scopy)
-        load_w(2)
+        v_widen(0, 1, 0, True)
+        v_widen(0, 1, 1, True)
+        v_widen(0, 1, 2, False)
+        v_widen(0, 1, 3, False)
         v_interleave(0, 0)
+        w_evac(0, 0, scopy)
         w_evac(0, 1, scopy)
-        v_widen(1, 1, 2, False)
-        load_w(3)
         w_flip(1, 0)
-        v_widen(1, 1, 3, False)
-        v_widen(1, 1, 0, True)
         w_flip(1, 1)
-        v_widen(1, 1, 1, True)
-        v_widen(1, 0, 2, False)
-        v_quant(0, 1)
-        load_v(2)
-        v_widen(1, 0, 3, False)
+        v_interleave(0, 1)
         v_widen(1, 0, 0, True)
         v_widen(1, 0, 1, True)
-        w_evac(1, 0, scopy)
+        v_widen(1, 0, 2, False)
+        v_widen(1, 0, 3, False)
         v_quant(0, 0)
-        w_flip(2, 0)
+        v_widen(1, 1, 0, True)
+        v_widen(1, 1, 1, True)
+        v_widen(1, 1, 2, False)
+        v_widen(1, 1, 3, False)
+        v_quant(0, 1)
+        w_evac(1, 0, scopy)
         w_evac(1, 1, scopy)
         load_w(4)
-        v_interleave(1, 1)
+        w_flip(2, 0)
         w_flip(2, 1)
         w_evac(2, 0, scopy)
-        w_flip(3, 0)
         w_evac(2, 1, scopy)
         load_w(5)
+        load_v(3)
         v_interleave(1, 0)
+        v_widen(2, 0, 0, True)
+        v_widen(2, 0, 1, True)
+        v_widen(2, 0, 2, False)
+        v_widen(2, 0, 3, False)
+        w_flip(3, 0)
         w_flip(3, 1)
         w_evac(3, 0, scopy)
-        flip_q(0)
         w_evac(3, 1, scopy)
-        flip_k(0)
-        load_w(6)
-        flip_k(1)
-        w_quant(0, 0)
-        v_widen(2, 1, 1, False)
-        flip_q(1)
-        v_widen(2, 1, 0, True)
-        v_widen(2, 1, 2, False)
-        load_v(3)
-        v_quant(1, 1)
-        v_widen(2, 1, 3, False)
-        v_widen(2, 0, 0, True)
-        v_widen(2, 0, 1, False)
+        v_interleave(1, 1)
         v_quant(1, 0)
-        load_w(7)
-        v_widen(2, 0, 2, False)
-        flop_k(0, vcopy)
-        flop_q(1, vcopy)
-        v_widen(2, 0, 3, False)
-        v_interleave(2, 1)
-        load_gate(0)
-        flop_q(0, scopy)
-        flop_k(1, scopy)
-        w_flip(4, 0)
+        v_widen(2, 1, 0, True)
+        v_widen(2, 1, 1, True)
+        v_widen(2, 1, 2, False)
+        v_widen(2, 1, 3, False)
+        w_quant(0, 0)
         w_quant(0, 1)
+        w_flip(4, 0)
         w_flip(4, 1)
-        load_x(0)
         w_evac(4, 0, scopy)
-        v_interleave(2, 0)
-        sim_mm(0, 0)
         w_evac(4, 1, scopy)
-        load_gate(1)
-        sim_mm(0, 1)
-        spread_bias()
+        load_w(6)
+        load_w(7)
+        load_gate(0)
+        v_quant(1, 1)
+        v_interleave(2, 0)
+        v_widen(3, 0, 0, True)
+        v_widen(3, 0, 1, True)
+        v_widen(3, 0, 2, False)
+        v_widen(3, 0, 3, False)
         w_flip(5, 0)
+        w_flip(5, 1)
+        w_evac(5, 0, scopy)
+        w_evac(5, 1, scopy)
+        v_interleave(2, 1)
+        v_quant(2, 0)
+        v_widen(3, 1, 0, True)
+        v_widen(3, 1, 1, True)
+        v_widen(3, 1, 2, False)
+        v_widen(3, 1, 3, False)
+        w_flip(6, 0)
+        w_flip(6, 1)
+        w_evac(6, 0, scopy)
+        w_evac(6, 1, scopy)
+        flip_q(0)
+        flip_k(0)
+        flip_k(1)
+        flip_q(1)
+        flop_q(0, scopy)
+        flop_k(0, scopy)
+        flop_k(1, scopy)
+        flop_q(1, scopy)
+        sim_mm(0, 0)
+        sim_mm(0, 1)
         relu(0, 0)
         relu(0, 1)
-        v_widen(3, 1, 0, True)
-        load_gate(2)
-        w_flip(5, 1)
-        v_widen(3, 1, 1, True)
-        w_evac(5, 0, scopy)
-        sim_mm(1, 0)
-        v_widen(3, 1, 2, True)
-        v_widen(3, 1, 3, True)
-        sim_mm(1, 1)
-        w_evac(5, 1, scopy)
-        v_quant(2, 1)
-        load_x(1)
-        make_xb(0)
-        w_flip(6, 0)
-        relu(1, 0)
-        v_widen(3, 0, 0, True)
-        load_gate(3)
-        w_flip(6, 1)
-        v_widen(3, 0, 1, True)
-        relu(1, 1)
-        v_widen(3, 0, 2, True)
-        sim_mm(2, 0)
-        v_widen(3, 0, 3, True)
         square(0)
-        v_quant(2, 0)
-        sim_mm(2, 1)
-        load_x(2)
-        w_quant(0, 2)
-        w_evac(6, 0, scopy)
-        v_interleave(3, 1)
-        make_xb(1)
-        w_evac(6, 1, scopy)
-        w_flip(7, 0)
-        relu(2, 0)
-        w_flip(7, 1)
-        a_quant(0)
-        relu(2, 1)
-        sim_mm(3, 0)
+        load_gate(1)
+        v_quant(2, 1)
         v_interleave(3, 0)
-        square(1)
-        sim_mm(3, 1)
-        mm1(0, 0)
-        v_quant(3, 1)
-        mm1(0, 1)
+        w_flip(7, 0)
+        w_flip(7, 1)
         w_evac(7, 0, scopy)
-        mm1(0, 2)
-        v_quant(3, 0)
         w_evac(7, 1, scopy)
-        a_quant(1)
-        relu(3, 0)
-        mm1(0, 3)
+        v_interleave(3, 1)
+        v_quant(3, 0)
+        v_quant(3, 1)
+        a_quant(0)
+        load_gate(2)
+        load_gate(3)
+        load_x(0)
+        load_x(1)
+        load_x(2)
+        sim_mm(1, 0)
+        sim_mm(1, 1)
+        relu(1, 0)
+        relu(1, 1)
+        square(1)
+        sim_mm(2, 0)
+        sim_mm(2, 1)
+        mm1(0, 0)
+        mm1(0, 1)
         gate_mul(0, 0)
-        relu(3, 1)
-        sim_mm(4, 0)
-        gate_mul(0, 1)
-        sim_mm(4, 1)
+        mm1(0, 2)
+        mm1(0, 3)
+        relu(2, 0)
+        relu(2, 1)
         square(2)
-        mm1(1, 0)
+        gate_mul(0, 1)
+        a_quant(1)
         gate_mul(0, 2)
-        mm1(1, 1)
         gate_mul(0, 3)
-        square(3)
-        mm1(1, 2)
-        a_quant(2)
-        load_gate(4)
-        gate_mul(1, 0)
-        mm1(1, 3)
-        gate_mul(1, 1)
-        v_flip(0, 1)
-        gate_mul(1, 2)
-        v_flip(0, 0)
-        v_evac(0, 1, scopy)
-        mm1(2, 0)
-        gate_mul(1, 3)
-        v_evac(0, 0, scopy)
-        mm1(2, 1)
+        w_quant(0, 2)
         w_quant(0, 3)
-        load_gate(5)
-        relu(4, 0)
-        mm1(2, 2)
-        a_quant(3)
-        relu(4, 1)
+        sim_mm(3, 0)
+        sim_mm(3, 1)
+        load_gate(4)
+        mm1(1, 0)
+        mm1(1, 1)
+        gate_mul(1, 0)
+        v_flip(0, 0)
+        v_flip(0, 1)
+        mm1(1, 2)
+        mm1(1, 3)
+        relu(3, 0)
+        relu(3, 1)
+        square(3)
+        v_evac(0, 0, scopy)
+        v_evac(0, 1, scopy)
+        gate_mul(1, 1)
+        a_quant(2)
+        gate_mul(1, 2)
+        gate_mul(1, 3)
         w_quant(1, 0)
-        mm1(2, 3)
-        load_x(3)
+        w_quant(1, 1)
+        sim_mm(4, 0)
+        sim_mm(4, 1)
+        spread_bias()
+        load_gate(5)
+        mm1(2, 0)
+        mm1(2, 1)
         gate_mul(2, 0)
+        v_flip(1, 0)
+        v_flip(1, 1)
+        mm1(2, 2)
+        mm1(2, 3)
+        relu(4, 0)
+        relu(4, 1)
         square(4)
+        v_evac(1, 0, scopy)
+        v_evac(1, 1, scopy)
+        gate_mul(2, 1)
+        a_quant(3)
+        gate_mul(2, 2)
+        v_t_quant(0)
+        gate_mul(2, 3)
+        w_quant(1, 2)
         sim_mm(5, 0)
         sim_mm(5, 1)
-        gate_mul(2, 1)
-        mm1(3, 0)
-        gate_mul(2, 2)
-        relu(5, 0)
-        v_flip(1, 1)
-        gate_mul(2, 3)
-        relu(5, 1)
-        v_flip(1, 0)
-        sim_mm(6, 0)
-        v_evac(1, 1, scopy)
-        v_t_quant(0)
+        make_xb(0, 0)
         load_gate(6)
-        sim_mm(6, 1)
-        v_evac(1, 0, scopy)
-        a_quant(4)
+        mm1(3, 0)
         mm1(3, 1)
-        w_quant(1, 1)
-        square(5)
-        load_x(4)
-        mm1(3, 2)
         gate_mul(3, 0)
-        mm1(3, 3)
-        gate_mul(3, 1)
-        relu(6, 0)
-        mm1(4, 0)
-        a_quant(5)
-        relu(6, 1)
-        sim_mm(7, 0)
-        w_quant(1, 2)
-        sim_mm(7, 1)
-        square(6)
-        gate_mul(3, 2)
-        mm1(4, 1)
-        v_t_quant(1)
-        v_flip(2, 1)
         v_flip(2, 0)
-        gate_mul(3, 3)
-        v_evac(2, 1, scopy)
-        mm1(4, 2)
-        gate_mul(4, 0)
-        relu(7, 0)
-        load_gate(7)
-        mm2(0, (0,))
-        w_quant(1, 3)
-        relu(7, 1)
-        a_quant(6)
+        v_flip(2, 1)
+        mm1(3, 2)
+        mm1(3, 3)
+        relu(5, 0)
+        relu(5, 1)
+        square(5)
         v_evac(2, 0, scopy)
-        gate_mul(4, 1)
-        mm2(0, (1,))
-        square(7)
-        gate_mul(4, 2)
-        finish(0, 0)
+        v_evac(2, 1, scopy)
+        gate_mul(3, 1)
+        a_quant(4)
+        gate_mul(3, 2)
+        v_t_quant(1)
+        gate_mul(3, 3)
+        w_quant(1, 3)
+        sim_mm(6, 0)
+        sim_mm(6, 1)
+        make_xb(0, 1)
+        load_x(3)
+        load_gate(7)
+        mm1(4, 0)
+        mm1(4, 1)
+        gate_mul(4, 0)
+        v_flip(3, 0)
+        v_flip(3, 1)
+        mm1(4, 2)
         mm1(4, 3)
-        finish(0, 1)
-        mm1(5, 0)
-        gate_mul(4, 3)
-        mm1(5, 1)
-        make_xb(2)
-        a_quant(7)
-        mm1(5, 2)
-        gate_mul(5, 0)
-        mm2(1, (0,))
+        relu(6, 0)
+        relu(6, 1)
+        square(6)
+        v_evac(3, 0, scopy)
+        v_evac(3, 1, scopy)
+        gate_mul(4, 1)
+        a_quant(5)
+        gate_mul(4, 2)
         v_t_quant(2)
-        gate_mul(5, 1)
-        mm2(1, (1,))
-        load_x(5)
-        gate_mul(5, 2)
-        finish(1, 0)
+        gate_mul(4, 3)
+        sim_mm(7, 0)
+        sim_mm(7, 1)
+        mm2(0, (0,))
+        finish(0, 0)
+        make_xb(1, 0)
+        mm1(5, 0)
+        mm1(5, 1)
+        gate_mul(5, 0)
+        v_flip(4, 0)
+        v_flip(4, 1)
+        mm1(5, 2)
         mm1(5, 3)
-        finish(1, 1)
-        mm1(6, 0)
+        relu(7, 0)
+        relu(7, 1)
+        square(7)
+        v_evac(4, 0, scopy)
+        v_evac(4, 1, scopy)
+        gate_mul(5, 1)
+        a_quant(6)
+        gate_mul(5, 2)
+        v_t_quant(3)
         gate_mul(5, 3)
-        make_xb(3)
+        mm2(0, (1,))
+        finish(0, 1)
+        mm2(1, (0,))
+        finish(1, 0)
+        make_xb(1, 1)
+        load_x(4)
+        make_xb(2, 0)
+        mm1(6, 0)
         mm1(6, 1)
         gate_mul(6, 0)
+        v_flip(5, 0)
+        v_flip(5, 1)
         mm1(6, 2)
-        gate_mul(6, 1)
         mm1(6, 3)
+        v_evac(5, 0, scopy)
+        v_evac(5, 1, scopy)
+        gate_mul(6, 1)
+        a_quant(7)
         gate_mul(6, 2)
-        v_flip(3, 1)
+        v_t_quant(4)
         gate_mul(6, 3)
-        v_flip(3, 0)
-        load_x(6)
-        v_evac(3, 1, scopy)
+        mm2(1, (1,))
+        finish(1, 1)
+        mm2(2, (0,))
+        finish(2, 0)
+        make_xb(2, 1)
+        load_x(5)
+        make_xb(3, 0)
         mm1(7, 0)
-        v_evac(3, 0, scopy)
         mm1(7, 1)
         gate_mul(7, 0)
-        mm2(2, (0,))
-        gate_mul(7, 1)
-        mm2(2, (1,))
-        finish(2, 0)
-        mm1(7, 2)
-        finish(2, 1)
-        mm1(7, 3)
-        gate_mul(7, 2)
-        make_xb(4)
-        v_flip(4, 1)
-        v_t_quant(3)
-        v_flip(4, 0)
-        v_evac(4, 1, scopy)
-        gate_mul(7, 3)
-        v_flip(5, 1)
-        v_flip(5, 0)
-        v_evac(4, 0, scopy)
-        v_evac(5, 1, vcopy)
-        mm2(3, (0,))
-        v_evac(5, 0, scopy)
-        v_t_quant(4)
-        load_x(7)
-        mm2(3, (1,))
-        finish(3, 0)
-        v_flip(6, 1)
-        finish(3, 1)
         v_flip(6, 0)
-        v_evac(6, 1, scopy)
-        v_t_quant(5)
-        v_flip(7, 1)
-        make_xb(5)
-        v_flip(7, 0)
+        v_flip(6, 1)
+        mm1(7, 2)
+        mm1(7, 3)
         v_evac(6, 0, scopy)
-        v_evac(7, 1, vcopy)
-        mm2(4, (0,))
+        v_evac(6, 1, scopy)
+        gate_mul(7, 1)
+        gate_mul(7, 2)
+        v_t_quant(5)
+        gate_mul(7, 3)
+        mm2(2, (1,))
+        finish(2, 1)
+        mm2(3, (0,))
+        finish(3, 0)
+        make_xb(3, 1)
+        load_x(6)
+        make_xb(4, 0)
+        v_flip(7, 0)
+        v_flip(7, 1)
         v_evac(7, 0, scopy)
+        v_evac(7, 1, vcopy)
         v_t_quant(6)
-        mm2(4, (1,))
-        finish(4, 0)
-        mm2(5, (0,))
-        finish(4, 1)
+        mm2(3, (1,))
+        finish(3, 1)
+        make_xb(4, 1)
+        load_x(7)
         v_t_quant(7)
-        make_xb(6)
-        mm2(5, (1,))
+        mm2(4, (0,))
+        finish(4, 0)
+        make_xb(5, 0)
+        mm2(4, (1,))
+        finish(4, 1)
+        make_xb(5, 1)
+        mm2(5, (0,))
         finish(5, 0)
-        mm2(6, (0,))
+        make_xb(6, 0)
+        mm2(5, (1,))
         finish(5, 1)
-        make_xb(7)
-        mm2(6, (1,))
+        make_xb(6, 1)
+        mm2(6, (0,))
         finish(6, 0)
-        mm2(7, (0,))
+        make_xb(7, 0)
+        mm2(6, (1,))
         finish(6, 1)
-        mm2(7, (1,))
+        make_xb(7, 1)
+        mm2(7, (0,))
         finish(7, 0)
+        mm2(7, (1,))
         finish(7, 1)

from contextlib import ExitStack

import concourse.mybir as mybir
from concourse.masks import make_identity

S, D, H, QK = 1024, 1024, 2048, 128
P = 128
F32 = mybir.dt.float32
BF16 = mybir.dt.bfloat16
U32 = mybir.dt.uint32
U8 = mybir.dt.uint8
FP8 = mybir.dt.float8_e4m3fn
X4 = mybir.dt.float8_e4m3fn_x4
ACT = mybir.ActivationFunctionType
ALU = mybir.AluOpType

FLOPS = 2 * S * S * QK + 2 * S * S * H + 2 * S * H * D

QT = S // P
KG = S // 512
HC = H // 512
DB = D // P


def tile_gau_pa_kernel(tc, q, k, v_bytes, v_scale, gate, W_out, b_out, x, out):
    nc = tc.nc
    with ExitStack() as ctx:
        const = ctx.enter_context(tc.tile_pool(name="const", bufs=1))
        keep = ctx.enter_context(tc.tile_pool(name="keep", bufs=1))
        work = ctx.enter_context(tc.tile_pool(name="work", bufs=2))
        psum = ctx.enter_context(tc.psum_pool(name="psum", bufs=4))
        ctx.enter_context(tc.manual_schedule())

        q_view = q.rearrange("b (p i) d -> p (b i) d", i=QT)
        k_view = k.rearrange("b (g m t) d -> m (b g) t d", g=KG, t=4)
        v_view = v_bytes.rearrange("b (g p t) n -> (b g) p t n", p=P, t=4)
        s_view = v_scale.rearrange("b (g p t) o -> p (b g) (t o)", p=P, t=4)
        gate_view = gate.rearrange("b (p i) h -> p (b i) h", i=QT)
        x_view = x.rearrange("b (p i) d -> p (b i) d", i=QT)
        out_view = out.rearrange("b (p i) d -> p (b i) d", i=QT)
        w_view = W_out.rearrange("(j p) h -> j p h", p=P)

        q_sb = const.tile([P, QT, QK], BF16, name="q_sb")
        k_sb = const.tile([P, KG, 4, QK], BF16, name="k_sb")
        v_sc = const.tile([P, KG, 4], F32, name="v_sc")
        b_row = const.tile([P, D], BF16, name="b_row")
        ident_b = const.tile([P, P], BF16, name="ident_b")
        ident_f = const.tile([P, P], F32, name="ident_f")
        ones = const.tile([P, P], BF16, name="ones")

        make_identity(nc, ident_b[:])
        make_identity(nc, ident_f[:])
        nc.gpsimd.memset(b_row[:], 0.0)
        nc.gpsimd.memset(ones[:], 1.0)
        warm = const.tile([P, 1], F32, name="warm")
        nc.vector.memset(warm[:], 0.0)
        nc.scalar.activation(out=warm[:], in_=warm[:], func=ACT.Square)


        v_raw = {}
        w_raw = {}
        gates = {}
        xs = {}

        def load_v(c):
            for g in range(KG):
                t = keep.tile([P, 4, 512], U8, name="v_raw_%d_%d" % (c, g), align_bytes=64)
                nc.sync.dma_start(out=t[:], in_=v_view[g][:, :, c * 512 : (c + 1) * 512])
                v_raw[c, g] = t

        def load_q():
            nc.sync.dma_start(out=q_sb[:], in_=q_view)

        def load_k():
            nc.sync.dma_start(out=k_sb[:], in_=k_view)

        nc.sync.dma_start(out=v_sc[:], in_=s_view)

        def load_w(j):
            t = work.tile([P, H], BF16, name="w_raw_%d" % j, tag="w_raw", bufs=4)
            nc.sync.dma_start(out=t[:], in_=w_view[j])
            w_raw[j] = t

        def load_gate(i):
            t = work.tile([P, H], BF16, name="gate_%d" % i, tag="gate", bufs=4)
            nc.sync.dma_start(out=t[:], in_=gate_view[:, i, :])
            gates[i] = t

        def load_x(i):
            t = work.tile([P, D], BF16, name="x_%d" % i, tag="x", bufs=3)
            nc.sync.dma_start(out=t[:], in_=x_view[:, i, :])
            xs[i] = t

        qT = const.tile([P, S], BF16, name="qT")
        kT = const.tile([P, S], BF16, name="kT")

        qk_ps = {}

        def flip_q(half):
            ps = psum.tile([P, 4, P], BF16, name="flip", tag="misc", bufs=4)
            for t in range(4):
                nc.tensor.transpose(ps[:, t, :], q_sb[:, 4 * half + t, :], ident_b[:])
            qk_ps["q", half] = ps

        def flip_k(half):
            ps = psum.tile([P, 4, P], BF16, name="flip", tag="misc", bufs=4)
            for t in range(4):
                nc.tensor.transpose(ps[:, t, :], k_sb[:, half, t, :], ident_b[:])
            qk_ps["k", half] = ps

        def flop_q(half, copy):
            copy(out=qT[:, half * 512 : (half + 1) * 512], in_=qk_ps["q", half][:].rearrange("p t m -> p (t m)"))

        def flop_k(half, copy):
            copy(out=kT[:, half * 512 : (half + 1) * 512], in_=qk_ps["k", half][:].rearrange("p t m -> p (t m)"))

        r_t = {}
        a_codes = {}
        a_scales = {}
        sims = {}

        def sim_mm(i, g):
            ps = psum.tile([P, 4, P], F32, name="sim", tag="misc", bufs=4)
            for t in range(4):
                o = (4 * g + t) * P
                nc.tensor.matmul(ps[:, t, :], lhsT=kT[:, o : o + P], rhs=qT[:, i * P : (i + 1) * P], start=True, stop=True)
            sims[i, g] = ps

        def relu(i, g):
            if i not in r_t:
                r_t[i] = work.tile([P, S], F32, name="r", tag="r", bufs=2)
            nc.scalar.activation(
                out=r_t[i][:, g * 512 : (g + 1) * 512].rearrange("p (q t) -> p q t", t=4),
                in_=sims[i, g][:].rearrange("p t q -> p q t"),
                func=ACT.Relu,
                scale=1.0 / S,
            )

        def square(i):
            a = work.tile([P, S], BF16, name="a", tag="a", bufs=2, align_bytes=64)
            nc.scalar.activation(out=a[:], in_=r_t[i][:], func=ACT.Square)
            r_t[i] = a

        def a_quant(i):
            c = keep.tile([P, KG * P], U32, name="a_codes_%d" % i, align_bytes=64)
            s = keep.tile([P, KG * P], U8, name="a_scales_%d" % i, align_bytes=64)
            nc.vector.quantize_mx(out=c[:].bitcast(X4), scales=s[:], in_=r_t[i][:])
            a_codes[i] = c
            a_scales[i] = s

        v_wide = {}
        v_il = {}
        v_codes = {}
        v_scales = {}

        def v_widen(c, g, t, on_vector):
            if (c, g) not in v_wide:
                v_wide[c, g] = work.tile([P, 4, 512], BF16, name="v_wide", tag="v_wide", bufs=3)
            w = v_wide[c, g]
            src = v_raw[c, g][:, t, :].bitcast(FP8)
            sc = v_sc[:, g, t : t + 1]
            if on_vector:
                nc.vector.tensor_scalar(out=w[:, t, :], in0=src, scalar1=sc, scalar2=None, op0=ALU.mult)
            else:
                nc.scalar.activation(out=w[:, t, :], in_=src, func=ACT.Copy, scale=sc)

        def v_interleave(c, g):
            t = work.tile([P, 2048], BF16, name="v_il", tag="v_il", bufs=2, align_bytes=64)
            nc.vector.tensor_copy(
                out=t[:].rearrange("p (c i t) -> p c t i", t=4, i=4),
                in_=v_wide[c, g][:].rearrange("p t (c i) -> p c t i", i=4),
            )
            v_il[c, g] = t

        def v_quant(c, g):
            co = keep.tile([P, 512], U32, name="v_codes_%d_%d" % (c, g), align_bytes=64)
            sc = keep.tile([P, 512], U8, name="v_scales_%d_%d" % (c, g), align_bytes=64)
            nc.vector.quantize_mx(out=co[:].bitcast(X4), scales=sc[:], in_=v_il[c, g][:])
            v_codes[c, g] = co
            v_scales[c, g] = sc

        w_il = {}
        w_codes = {}
        w_scales = {}

        w_ps = {}

        def w_flip(j, pair):
            words = w_raw[j][:].bitcast(F32)
            ps = psum.tile([P, 4, P], F32, name="w_flip", tag="misc", bufs=4)
            for c2 in range(2):
                for u in range(2):
                    base = 256 * (2 * pair + c2)
                    nc.tensor.transpose(ps[:, 2 * c2 + u, :], words[:, base + u : base + 256 : 2], ident_f[:])
            w_ps[j, pair] = ps

        def w_evac(j, pair, copy):
            half, jj = divmod(j, 4)
            if (half, pair) not in w_il:
                w_il[half, pair] = work.tile([P, 2 * 512 * 4], BF16, name="w_il", tag="w_il", bufs=3, align_bytes=64)
            dst = w_il[half, pair][:].bitcast(F32).rearrange("p (c d u) -> p c d u", c=2, u=2)[:, :, jj * P : (jj + 1) * P, :]
            copy(out=dst, in_=w_ps[j, pair][:].rearrange("p (c u) d -> p c d u", u=2))

        def w_quant(half, c):
            co = keep.tile([P, 512], U32, name="w_codes_%d_%d" % (half, c), align_bytes=64)
            sc = keep.tile([P, 512], U8, name="w_scales_%d_%d" % (half, c), align_bytes=64)
            src = w_il[half, c // 2][:, (c % 2) * 2048 : (c % 2 + 1) * 2048]
            nc.vector.quantize_mx(out=co[:].bitcast(X4), scales=sc[:], in_=src)
            w_codes[half, c] = co
            w_scales[half, c] = sc

        vb = {}
        accs = {}

        def mm1(i, c):
            acc = psum.tile([P, 512], F32, name="acc", tag="acc", bufs=4)
            for g in range(KG):
                cols = slice(g * P, (g + 1) * P)
                nc.tensor.matmul_mx(
                    out=acc[:],
                    lhsT=a_codes[i][:, cols].bitcast(X4),
                    lhsT_scale=a_scales[i][:, cols],
                    rhs=v_codes[c, g][:].bitcast(X4),
                    rhs_scale=v_scales[c, g][:],
                    start=(g == 0),
                    stop=(g == KG - 1),
                )
            accs[i, c] = acc

        def gate_mul(i, c):
            if i not in vb:
                vb[i] = work.tile([P, H], BF16, name="vb", tag="vb", bufs=3)
            cols = slice(c * 512, (c + 1) * 512)
            nc.vector.tensor_tensor(
                out=vb[i][:, cols].rearrange("p (u w e) -> p u w e", u=2, e=2),
                in0=accs[i, c][:].rearrange("p (w u e) -> p u w e", u=2, e=2),
                in1=gates[i][:, cols].rearrange("p (w u e) -> p u w e", u=2, e=2),
                op=ALU.mult,
            )

        vg = {}
        vt_codes = {}
        vt_scales = {}

        vps = {}

        def v_flip(i, pair):
            words = vb[i][:].bitcast(F32)
            ps = psum.tile([P, 4, P], F32, name="v_flip", tag="misc", bufs=4)
            for n in range(4):
                base = (4 * pair + n) * P
                nc.tensor.transpose(ps[:, n, :], words[:, base : base + P], ident_f[:])
            vps[i, pair] = ps

        def v_evac(i, pair, copy):
            if i not in vg:
                vg[i] = work.tile([P, H], BF16, name="vg", tag="vg", bufs=2, align_bytes=64)
            dst = vg[i][:].bitcast(F32).rearrange("p (c q u) -> p c q u", c=HC, u=2)
            copy(out=dst[:, 2 * pair : 2 * pair + 2], in_=vps[i, pair][:].rearrange("p (c u) q -> p c q u", u=2))

        def v_t_quant(i):
            co = work.tile([P, 512], U32, name="vt_codes", tag="vt_codes", bufs=8, align_bytes=64)
            sc = work.tile([P, 512], U8, name="vt_scales", tag="vt_scales", bufs=8, align_bytes=64)
            nc.vector.quantize_mx(out=co[:].bitcast(X4), scales=sc[:], in_=vg[i][:])
            vt_codes[i] = co
            vt_scales[i] = sc

        xb = {}
        outs = {}

        def make_xb(i, half):
            cols = slice(half * 512, (half + 1) * 512)
            xb[i, half] = work.tile([P, 512], F32, name="xb", tag="xb", bufs=4)
            nc.vector.tensor_tensor(out=xb[i, half][:], in0=xs[i][:, cols], in1=b_all[:, cols], op=ALU.add)

        def mm2(i, halves=(0, 1)):
            for half in halves:
                acc = psum.tile([P, 512], F32, name="acc", tag="acc", bufs=4)
                for c in range(HC):
                    cols = slice(c * P, (c + 1) * P)
                    nc.tensor.matmul_mx(
                        out=acc[:],
                        lhsT=vt_codes[i][:, cols].bitcast(X4),
                        lhsT_scale=vt_scales[i][:, cols],
                        rhs=w_codes[half, c][:].bitcast(X4),
                        rhs_scale=w_scales[half, c][:],
                        start=(c == 0),
                        stop=(c == HC - 1),
                    )
                outs[i, half] = acc

        o_t = {}

        def finish(i, half):
            cols = slice(half * 512, (half + 1) * 512)
            o = work.tile([P, 512], F32, name="o", tag="o", bufs=5)
            nc.vector.tensor_tensor(out=o[:], in0=outs[i, half][:], in1=xb[i, half][:], op=ALU.add)
            nc.sync.dma_start(out=out_view[:, i, cols], in_=o[:])

        vcopy = nc.vector.tensor_copy
        scopy = nc.scalar.copy
        b_all = const.tile([P, D], BF16, name="b_all")

        def spread_bias():
            for half in range(2):
                cols = slice(half * 512, (half + 1) * 512)
                ps = psum.tile([P, 512], F32, name="bias", tag="acc", bufs=4)
                nc.tensor.matmul(ps[:], lhsT=ones[:], rhs=b_row[:, cols], start=True, stop=True)
                nc.scalar.copy(out=b_all[:, cols], in_=ps[:])

        def load_bias():
            nc.sync.dma_start(out=b_row[0:1, :], in_=b_out.rearrange("(o d) -> o d", o=1))

        load_w(0)
        load_v(0)
        load_bias()
        load_w(1)
        load_v(1)
        load_w(2)
        load_w(3)
        load_v(2)
        load_q()
        load_k()
        w_flip(0, 0)
        w_flip(0, 1)
        v_widen(0, 0, 0, True)
        v_widen(0, 0, 1, True)
        v_widen(0, 0, 2, False)
        v_widen(0, 0, 3, False)
        v_widen(0, 1, 0, True)
        v_widen(0, 1, 1, True)
        v_widen(0, 1, 2, False)
        v_widen(0, 1, 3, False)
        v_interleave(0, 0)
        w_evac(0, 0, scopy)
        w_evac(0, 1, scopy)
        w_flip(1, 0)
        w_flip(1, 1)
        v_interleave(0, 1)
        v_widen(1, 0, 0, True)
        v_widen(1, 0, 1, True)
        v_widen(1, 0, 2, False)
        v_widen(1, 0, 3, False)
        v_quant(0, 0)
        v_widen(1, 1, 0, True)
        v_widen(1, 1, 1, True)
        v_widen(1, 1, 2, False)
        v_widen(1, 1, 3, False)
        v_quant(0, 1)
        w_evac(1, 0, scopy)
        w_evac(1, 1, scopy)
        load_w(4)
        w_flip(2, 0)
        w_flip(2, 1)
        w_evac(2, 0, scopy)
        w_evac(2, 1, scopy)
        load_w(5)
        load_v(3)
        v_interleave(1, 0)
        v_widen(2, 0, 0, True)
        v_widen(2, 0, 1, True)
        v_widen(2, 0, 2, False)
        v_widen(2, 0, 3, False)
        w_flip(3, 0)
        w_flip(3, 1)
        w_evac(3, 0, scopy)
        w_evac(3, 1, scopy)
        v_interleave(1, 1)
        v_quant(1, 0)
        v_widen(2, 1, 0, True)
        v_widen(2, 1, 1, True)
        v_widen(2, 1, 2, False)
        v_widen(2, 1, 3, False)
        w_quant(0, 0)
        w_quant(0, 1)
        w_flip(4, 0)
        w_flip(4, 1)
        w_evac(4, 0, scopy)
        w_evac(4, 1, scopy)
        load_w(6)
        load_w(7)
        load_gate(0)
        v_quant(1, 1)
        v_interleave(2, 0)
        v_widen(3, 0, 0, True)
        v_widen(3, 0, 1, True)
        v_widen(3, 0, 2, False)
        v_widen(3, 0, 3, False)
        w_flip(5, 0)
        w_flip(5, 1)
        w_evac(5, 0, scopy)
        w_evac(5, 1, scopy)
        v_interleave(2, 1)
        v_quant(2, 0)
        v_widen(3, 1, 0, True)
        v_widen(3, 1, 1, True)
        v_widen(3, 1, 2, False)
        v_widen(3, 1, 3, False)
        w_flip(6, 0)
        w_flip(6, 1)
        w_evac(6, 0, scopy)
        w_evac(6, 1, scopy)
        flip_q(0)
        flip_k(0)
        flip_k(1)
        flip_q(1)
        flop_q(0, scopy)
        flop_k(0, scopy)
        flop_k(1, scopy)
        flop_q(1, scopy)
        sim_mm(0, 0)
        sim_mm(0, 1)
        relu(0, 0)
        relu(0, 1)
        square(0)
        load_gate(1)
        v_quant(2, 1)
        v_interleave(3, 0)
        w_flip(7, 0)
        w_flip(7, 1)
        w_evac(7, 0, scopy)
        w_evac(7, 1, scopy)
        v_interleave(3, 1)
        v_quant(3, 0)
        v_quant(3, 1)
        a_quant(0)
        load_gate(2)
        load_gate(3)
        load_x(0)
        load_x(1)
        load_x(2)
        sim_mm(1, 0)
        sim_mm(1, 1)
        relu(1, 0)
        relu(1, 1)
        square(1)
        sim_mm(2, 0)
        sim_mm(2, 1)
        mm1(0, 0)
        mm1(0, 1)
        gate_mul(0, 0)
        mm1(0, 2)
        mm1(0, 3)
        relu(2, 0)
        relu(2, 1)
        square(2)
        gate_mul(0, 1)
        a_quant(1)
        gate_mul(0, 2)
        gate_mul(0, 3)
        w_quant(0, 2)
        w_quant(0, 3)
        sim_mm(3, 0)
        sim_mm(3, 1)
        load_gate(4)
        mm1(1, 0)
        mm1(1, 1)
        gate_mul(1, 0)
        v_flip(0, 0)
        v_flip(0, 1)
        mm1(1, 2)
        mm1(1, 3)
        relu(3, 0)
        relu(3, 1)
        square(3)
        v_evac(0, 0, scopy)
        v_evac(0, 1, scopy)
        gate_mul(1, 1)
        a_quant(2)
        gate_mul(1, 2)
        gate_mul(1, 3)
        w_quant(1, 0)
        w_quant(1, 1)
        sim_mm(4, 0)
        sim_mm(4, 1)
        spread_bias()
        load_gate(5)
        mm1(2, 0)
        mm1(2, 1)
        gate_mul(2, 0)
        v_flip(1, 0)
        v_flip(1, 1)
        mm1(2, 2)
        mm1(2, 3)
        relu(4, 0)
        relu(4, 1)
        square(4)
        v_evac(1, 0, scopy)
        v_evac(1, 1, scopy)
        gate_mul(2, 1)
        a_quant(3)
        gate_mul(2, 2)
        v_t_quant(0)
        gate_mul(2, 3)
        w_quant(1, 2)
        sim_mm(5, 0)
        sim_mm(5, 1)
        make_xb(0, 0)
        load_gate(6)
        mm1(3, 0)
        mm1(3, 1)
        gate_mul(3, 0)
        v_flip(2, 0)
        v_flip(2, 1)
        mm1(3, 2)
        mm1(3, 3)
        relu(5, 0)
        relu(5, 1)
        square(5)
        v_evac(2, 0, scopy)
        v_evac(2, 1, scopy)
        gate_mul(3, 1)
        a_quant(4)
        gate_mul(3, 2)
        v_t_quant(1)
        gate_mul(3, 3)
        w_quant(1, 3)
        sim_mm(6, 0)
        sim_mm(6, 1)
        make_xb(0, 1)
        load_x(3)
        load_gate(7)
        mm1(4, 0)
        mm1(4, 1)
        gate_mul(4, 0)
        v_flip(3, 0)
        v_flip(3, 1)
        mm1(4, 2)
        mm1(4, 3)
        relu(6, 0)
        relu(6, 1)
        square(6)
        v_evac(3, 0, scopy)
        v_evac(3, 1, scopy)
        gate_mul(4, 1)
        a_quant(5)
        gate_mul(4, 2)
        v_t_quant(2)
        gate_mul(4, 3)
        sim_mm(7, 0)
        sim_mm(7, 1)
        mm2(0, (0,))
        finish(0, 0)
        make_xb(1, 0)
        mm1(5, 0)
        mm1(5, 1)
        gate_mul(5, 0)
        v_flip(4, 0)
        v_flip(4, 1)
        mm1(5, 2)
        mm1(5, 3)
        relu(7, 0)
        relu(7, 1)
        square(7)
        v_evac(4, 0, scopy)
        v_evac(4, 1, scopy)
        gate_mul(5, 1)
        a_quant(6)
        gate_mul(5, 2)
        v_t_quant(3)
        gate_mul(5, 3)
        mm2(0, (1,))
        finish(0, 1)
        mm2(1, (0,))
        finish(1, 0)
        make_xb(1, 1)
        load_x(4)
        make_xb(2, 0)
        mm1(6, 0)
        mm1(6, 1)
        gate_mul(6, 0)
        v_flip(5, 0)
        v_flip(5, 1)
        mm1(6, 2)
        mm1(6, 3)
        v_evac(5, 0, scopy)
        v_evac(5, 1, scopy)
        gate_mul(6, 1)
        a_quant(7)
        gate_mul(6, 2)
        v_t_quant(4)
        gate_mul(6, 3)
        mm2(1, (1,))
        finish(1, 1)
        mm2(2, (0,))
        finish(2, 0)
        make_xb(2, 1)
        load_x(5)
        make_xb(3, 0)
        mm1(7, 0)
        mm1(7, 1)
        gate_mul(7, 0)
        v_flip(6, 0)
        v_flip(6, 1)
        mm1(7, 2)
        mm1(7, 3)
        v_evac(6, 0, scopy)
        v_evac(6, 1, scopy)
        gate_mul(7, 1)
        gate_mul(7, 2)
        v_t_quant(5)
        gate_mul(7, 3)
        mm2(2, (1,))
        finish(2, 1)
        mm2(3, (0,))
        finish(3, 0)
        make_xb(3, 1)
        load_x(6)
        make_xb(4, 0)
        v_flip(7, 0)
        v_flip(7, 1)
        v_evac(7, 0, scopy)
        v_evac(7, 1, vcopy)
        v_t_quant(6)
        mm2(3, (1,))
        finish(3, 1)
        make_xb(4, 1)
        load_x(7)
        v_t_quant(7)
        mm2(4, (0,))
        finish(4, 0)
        make_xb(5, 0)
        mm2(4, (1,))
        finish(4, 1)
        make_xb(5, 1)
        mm2(5, (0,))
        finish(5, 0)
        make_xb(6, 0)
        mm2(5, (1,))
        finish(5, 1)
        make_xb(6, 1)
        mm2(6, (0,))
        finish(6, 0)
        make_xb(7, 0)
        mm2(6, (1,))
        finish(6, 1)
        make_xb(7, 1)
        mm2(7, (0,))
        finish(7, 0)
        mm2(7, (1,))
        finish(7, 1)
